import numpy as np
import ml_dtypes


def mxq(x, axis, fmt="e4m3"):
    dtype, down = {"e4m3": (ml_dtypes.float8_e4m3fn, 7), "e5m2": (ml_dtypes.float8_e5m2, 14)}[fmt]
    v = np.moveaxis(np.asarray(x, np.float32).astype(ml_dtypes.bfloat16).astype(np.float64), axis, -1)
    blocks = v.reshape(v.shape[:-1] + (-1, 32))
    amax = np.abs(blocks).max(-1, keepdims=True)
    byte = np.maximum(np.where(amax > 0, np.frexp(amax)[1] - 1 + 127, 0) - down, 1)
    scale = np.exp2(byte - 127.0)
    codes = (blocks / scale).astype(np.float32).astype(dtype).astype(np.float64)
    return np.moveaxis((codes * scale).reshape(v.shape), -1, axis)


WIDE = False


def mx_kscale(k):
    if not WIDE:
        return np.ones(k)
    levels = np.array([10, -10, 5, -5, 0])
    a = np.random.permutation(np.resize(levels, k // 512 * 4)).reshape(k // 512, 4)
    idx = np.arange(k)
    return np.exp2(a[idx // 512, idx % 128 // 32])


BF16 = ml_dtypes.bfloat16


def bf(x):
    return np.asarray(x, np.float32).astype(BF16)


def f64(x):
    return np.asarray(x).astype(np.float64)


E2M1 = np.array([0.0, 0.5, 1.0, 1.5, 2.0, 3.0, 4.0, 6.0, -0.0, -0.5, -1.0, -1.5, -2.0, -3.0, -4.0, -6.0])


def pack_weight(w, fmt):
    k, n = w.shape
    w = f64(bf(w)).reshape(k // 32, 32, n)
    amax = np.abs(w).max(1)
    if fmt == "e4m3":
        byte = np.frexp(amax)[1] - 1 + 127 - 7
    else:
        mant, ex = np.frexp(amax / 6.0)
        byte = np.where(mant > 0.5, ex, ex - 1) + 127
    byte = np.clip(np.where(amax > 0, byte, 1), 1, 254)
    scaled = (w * np.exp2(127.0 - byte)[:, None, :]).reshape(k, n).astype(np.float32)
    by_word = np.ascontiguousarray(scaled.reshape(k // 512, 128, 4, n).transpose(0, 1, 3, 2))
    if fmt == "e4m3":
        words = by_word.astype(ml_dtypes.float8_e4m3fn).view(np.uint8)
    else:
        c = by_word.astype(ml_dtypes.float4_e2m1fn).view(np.uint8) & 0xF
        words = c[..., 0::2] | (c[..., 1::2] << 4)
    return np.ascontiguousarray(words), np.ascontiguousarray(byte.astype(np.uint8).reshape(k // 512, 16, n))


def unpack_weight(words, scales, fmt):
    g, p, n, _ = words.shape
    if fmt == "e4m3":
        vals = np.ascontiguousarray(words).view(ml_dtypes.float8_e4m3fn).astype(np.float64)
    else:
        nib = np.empty((g, p, n, 4), np.uint8)
        nib[..., 0::2] = words & 0xF
        nib[..., 1::2] = words >> 4
        vals = E2M1[nib]
    vals = vals * np.repeat(np.exp2(scales.astype(np.float64) - 127.0), 8, axis=1)[..., None]
    return vals.transpose(0, 1, 3, 2).reshape(g * 512, n)


B, S, F, U = 1, 128, 4096, 2048
K = 2 * F
TWO_PI = 2.0 * np.pi


def setup_inputs():
    s = mx_kscale(K)[:F]
    u = s / s.max()
    r = np.minimum(1.0, 8.0 * u)
    g = np.concatenate([r, r * r])
    x = bf(np.random.standard_normal((B, S, F)) * u)
    W_words, W_scales = pack_weight(np.random.standard_normal((K, U)) / np.sqrt(K) / g[:, None], "e4m3")
    b = bf(np.random.standard_normal(U) * 0.1)
    return {"x": x, "W_words": W_words, "W_scales": W_scales, "b": b}


def reference(x, W_words, W_scales, b):
    qp = f64(x) * TWO_PI
    quantum_enhanced = np.tanh(qp) + 0.1 * (np.sin(qp) * np.cos(qp * 0.5))
    entanglement = quantum_enhanced * quantum_enhanced
    feats = np.concatenate([quantum_enhanced, entanglement], axis=-1)
    return np.tanh((mxq(feats, 2, "e4m3") @ unpack_weight(W_words, W_scales, "e4m3")) + f64(b))

@@ -1,0 +1,179 @@
+import math
+from contextlib import ExitStack
+
+import concourse.mybir as mybir
+from concourse.masks import make_identity
+
+FLOPS = 2 * 128 * 8192 * 2048
+
+FP8X4 = mybir.dt.float8_e4m3fn_x4
+BF16 = mybir.dt.bfloat16
+F32 = mybir.dt.float32
+I32 = mybir.dt.int32
+U32 = mybir.dt.uint32
+U8 = mybir.dt.uint8
+ACT = mybir.ActivationFunctionType
+ALU = mybir.AluOpType
+
+P = 128
+TOK = 128
+F = 4096
+U = 2048
+NT = 512
+NCH = 4
+CW = 1024
+SCALES_PER_W = 3
+
+
+def tile_quantumprocessinglayer_w_kernel(tc, x, W_words, W_scales, b, out):
+    nc = tc.nc
+    with ExitStack() as ctx:
+        const = ctx.enter_context(tc.tile_pool(name="const", bufs=1))
+        wpool = ctx.enter_context(tc.tile_pool(name="wpool", bufs=1))
+        xgp = ctx.enter_context(tc.tile_pool(name="xgp", bufs=4))
+        tmp = ctx.enter_context(tc.tile_pool(name="tmp", bufs=2))
+        accp = ctx.enter_context(tc.psum_pool(name="accp", bufs=1))
+        tpp = ctx.enter_context(tc.psum_pool(name="tpp", bufs=4))
+        ctx.enter_context(tc.manual_schedule())
+
+        warm = const.tile([P, 1], F32, name="warm")
+        warm_out = const.tile([P, 1], F32, name="warm_out")
+        brow = const.tile([P, U], BF16, name="brow")
+        ones = const.tile([P, P], BF16, name="ones")
+        planes = const.tile([P, NCH, U], U8, name="planes", align_bytes=64)
+        ident = const.tile([P, P], F32, name="ident")
+        x_sb = const.tile([P, F], BF16, name="x_sb")
+        bias_sb = const.tile([P, U], F32, name="bias_sb")
+        codes = const.tile([P, NCH, 512], U32, name="codes", align_bytes=64)
+        fsc = const.tile([P, NCH, 512], U8, name="fsc", align_bytes=64)
+
+        nc.sync.dma_start(out=x_sb[:], in_=x[0])
+        nc.vector.memset(brow[:].bitcast(I32), 0)
+        nc.vector.memset(warm[:], 0.0)
+        nc.vector.memset(ones[:], 1.0)
+        nc.vector.memset(planes[:].rearrange("p c n -> p (c n)").bitcast(I32), 0)
+        nc.scalar.dma_start(out=brow[0:1, :], in_=b.unsqueeze(0))
+        nc.scalar.activation(out=warm_out[:], in_=warm[:], func=ACT.Silu)
+        make_identity(nc, ident[:])
+
+        w_tiles = {}
+
+        def load_w(g):
+            wt = wpool.tile([P, U], U32, name="w%d" % g, align_bytes=64)
+            nc.sync.dma_start(
+                out=wt[:].bitcast(I32),
+                in_=W_words[g].rearrange("p n t -> p (n t)").bitcast(I32),
+            )
+            for j in range(4):
+                w_tiles[(g, j)] = wt[:, NT * j : NT * (j + 1)]
+
+        def load_w_piece(g, j):
+            wt = wpool.tile([P, NT], U32, name="w%d_%d" % (g, j), align_bytes=64)
+            nc.sync.dma_start(
+                out=wt[:].bitcast(I32),
+                in_=W_words[g][:, NT * j : NT * (j + 1), :].rearrange("p n t -> p (n t)").bitcast(I32),
+            )
+            w_tiles[(g, j)] = wt[:]
+
+        def load_scales(c, q4):
+            nc.sync.dma_start(
+                out=planes[32 * q4 : 32 * q4 + 16, c, :].bitcast(I32),
+                in_=W_scales[c::4, 4 * q4 : 4 * q4 + 4, :].bitcast(I32),
+            )
+
+        g_order = [c + 4 * a for c in range(NCH) for a in range(4)]
+        s_order = [(c, q4) for c in range(NCH) for q4 in (0, 2, 1, 3)]
+        si = 0
+        for i, g in enumerate(g_order):
+            if i == len(g_order) - 1:
+                for j in range(4):
+                    load_w_piece(g, j)
+            else:
+                load_w(g)
+            if i >= 1:
+                for r in range(SCALES_PER_W):
+                    if si < len(s_order):
+                        load_scales(s_order[si][0], s_order[si][1])
+                        si += 1
+
+        for j in range(4):
+            bp = accp.tile([P, NT], F32, name="bp%d" % j, tag="acc%d" % j)
+            nc.tensor.matmul(bp[:], lhsT=ones[:], rhs=brow[:, NT * j : NT * (j + 1)], start=True, stop=True)
+            nc.scalar.copy(out=bias_sb[:, NT * j : NT * (j + 1)], in_=bp[:])
+
+        xw = x_sb[:].bitcast(F32)
+        xts = []
+        for c in range(NCH):
+            xt = tpp.tile([P, 2, 2, TOK], F32, name="xt%d" % c, tag="xt")
+            for gi in range(2):
+                g = c + 4 * gi
+                for u in range(2):
+                    nc.tensor.transpose(xt[:, gi, u, :], xw[:, 256 * g + u : 256 * (g + 1) : 2], ident[:])
+            xts.append(xt)
+
+        st = {}
+
+        def front(c):
+            xg = xgp.tile([P, 2, TOK, 2], F32, name="xg%d" % c, tag="xg")
+            nc.vector.tensor_copy(out=xg[:], in_=xts[c][:].rearrange("p g u r -> p g r u"))
+            xb = xg[:].rearrange("p g r u -> p (g r u)").bitcast(BF16)
+            t_t = tmp.tile([P, CW], F32, name="t%d" % c, tag="t")
+            nc.scalar.activation(out=t_t[:], in_=xb, func=ACT.Tanh, scale=2.0 * math.pi)
+            k_t = tmp.tile([P, CW], I32, name="k%d" % c, tag="k")
+            nc.vector.tensor_scalar(out=k_t[:], in0=xb, scalar1=0.5, scalar2=None, op0=ALU.mult)
+            xr = tmp.tile([P, CW], BF16, name="xr%d" % c, tag="xr")
+            nc.vector.scalar_tensor_tensor(out=xr[:], in0=k_t[:], scalar=-2.0, in1=xb, op0=ALU.mult, op1=ALU.add)
+            s_t = tmp.tile([P, CW], F32, name="s%d" % c, tag="s")
+            nc.scalar.activation(out=s_t[:], in_=xr[:], func=ACT.Sin, scale=math.pi)
+            s2 = tmp.tile([P, CW], F32, name="ss%d" % c, tag="ss")
+            nc.scalar.activation(out=s2[:], in_=s_t[:], func=ACT.Square)
+            st[c] = (t_t, s_t, s2)
+
+        def back_a(c):
+            t_t, s_t, s2 = st[c]
+            nc.vector.scalar_tensor_tensor(out=s2[:], in0=s2[:], scalar=1.0, in1=s_t[:], op0=ALU.subtract, op1=ALU.mult)
+            nc.vector.scalar_tensor_tensor(out=t_t[:], in0=s2[:], scalar=-0.2, in1=t_t[:], op0=ALU.mult, op1=ALU.add)
+            fb = tmp.tile([P, 2 * CW], BF16, name="fb%d" % c, tag="fb", align_bytes=64)
+            nc.vector.tensor_copy(out=fb[:, 0:CW], in_=t_t[:])
+            nc.scalar.activation(out=fb[:, CW : 2 * CW], in_=t_t[:], func=ACT.Square)
+            st[c] = fb
+
+        accs = []
+
+        def back_b(c):
+            fb = st[c]
+            nc.vector.quantize_mx(out=codes[:, c, :].bitcast(FP8X4), scales=fsc[:, c, :], in_=fb[:])
+            if c == 0:
+                for j in range(4):
+                    accs.append(accp.tile([P, NT], F32, name="acc%d" % j, tag="acc%d" % j))
+            for a in range(4):
+                g = c + 4 * a
+                for j in range(4):
+                    nc.tensor.matmul_mx(
+                        out=accs[j][:],
+                        lhsT=codes[:, c, P * a : P * (a + 1)].bitcast(FP8X4),
+                        lhsT_scale=fsc[:, c, P * a : P * (a + 1)],
+                        rhs=w_tiles[(g, j)].bitcast(FP8X4),
+                        rhs_scale=planes[4 * a : P, c, NT * j : NT * (j + 1)],
+                        start=(c == 0 and a == 0),
+                        stop=(c == NCH - 1 and a == 3),
+                    )
+
+        front(0)
+        front(1)
+        back_a(0)
+        front(2)
+        back_b(0)
+        back_a(1)
+        front(3)
+        back_b(1)
+        back_a(2)
+        back_b(2)
+        back_a(3)
+        back_b(3)
+
+        for j in range(4):
+            js = slice(NT * j, NT * (j + 1))
+            nc.vector.tensor_tensor(out=bias_sb[:, js], in0=accs[j][:], in1=bias_sb[:, js], op=ALU.add)
+            nc.scalar.activation(out=bias_sb[:, js], in_=bias_sb[:, js], func=ACT.Tanh)
+            nc.sync.dma_start(out=out[0][:, js], in_=bias_sb[:, js])

@@ -96,11 +96,6 @@ def tile_quantumprocessinglayer_w_kernel(tc, x, W_words, W_scales, b, out):
                         load_scales(s_order[si][0], s_order[si][1])
                         si += 1
 
-        for j in range(4):
-            bp = accp.tile([P, NT], F32, name="bp%d" % j, tag="acc%d" % j)
-            nc.tensor.matmul(bp[:], lhsT=ones[:], rhs=brow[:, NT * j : NT * (j + 1)], start=True, stop=True)
-            nc.scalar.copy(out=bias_sb[:, NT * j : NT * (j + 1)], in_=bp[:])
-
         xw = x_sb[:].bitcast(F32)
         xts = []
         for c in range(NCH):
@@ -113,10 +108,19 @@ def tile_quantumprocessinglayer_w_kernel(tc, x, W_words, W_scales, b, out):
 
         st = {}
 
-        def front(c):
+        xgs = {}
+
+        def copy_out(c, eng):
             xg = xgp.tile([P, 2, TOK, 2], F32, name="xg%d" % c, tag="xg")
-            nc.vector.tensor_copy(out=xg[:], in_=xts[c][:].rearrange("p g u r -> p g r u"))
-            xb = xg[:].rearrange("p g r u -> p (g r u)").bitcast(BF16)
+            src_ap = xts[c][:].rearrange("p g u r -> p g r u")
+            if eng == "v":
+                nc.vector.tensor_copy(out=xg[:], in_=src_ap)
+            else:
+                nc.scalar.copy(out=xg[:], in_=src_ap)
+            xgs[c] = xg[:].rearrange("p g r u -> p (g r u)").bitcast(BF16)
+
+        def front(c):
+            xb = xgs[c]
             t_t = tmp.tile([P, CW], F32, name="t%d" % c, tag="t")
             nc.scalar.activation(out=t_t[:], in_=xb, func=ACT.Tanh, scale=2.0 * math.pi)
             k_t = tmp.tile([P, CW], I32, name="k%d" % c, tag="k")
@@ -159,7 +163,16 @@ def tile_quantumprocessinglayer_w_kernel(tc, x, W_words, W_scales, b, out):
                         stop=(c == NCH - 1 and a == 3),
                     )
 
+        copy_out(0, "v")
+        copy_out(1, "s")
         front(0)
+        copy_out(2, "v")
+        copy_out(3, "s")
+        bps = []
+        for j in range(4):
+            bp = tpp.tile([P, NT], F32, name="bp%d" % j, tag="xt")
+            nc.tensor.matmul(bp[:], lhsT=ones[:], rhs=brow[:, NT * j : NT * (j + 1)], start=True, stop=True)
+            bps.append(bp)
         front(1)
         back_a(0)
         front(2)
@@ -171,6 +184,8 @@ def tile_quantumprocessinglayer_w_kernel(tc, x, W_words, W_scales, b, out):
         back_b(2)
         back_a(3)
         back_b(3)
+        for j in range(4):
+            nc.scalar.copy(out=bias_sb[:, NT * j : NT * (j + 1)], in_=bps[j][:])
 
         for j in range(4):
             js = slice(NT * j, NT * (j + 1))

@@ -23,6 +23,7 @@ NT = 512
 NCH = 4
 CW = 1024
 SCALES_PER_W = 3
+RANGES = [(0, 512), (512, 512), (1024, 512), (1536, 256), (1792, 256)]
 
 
 def tile_quantumprocessinglayer_w_kernel(tc, x, W_words, W_scales, b, out):
@@ -33,7 +34,7 @@ def tile_quantumprocessinglayer_w_kernel(tc, x, W_words, W_scales, b, out):
         xgp = ctx.enter_context(tc.tile_pool(name="xgp", bufs=4))
         tmp = ctx.enter_context(tc.tile_pool(name="tmp", bufs=2))
         accp = ctx.enter_context(tc.psum_pool(name="accp", bufs=1))
-        tpp = ctx.enter_context(tc.psum_pool(name="tpp", bufs=4))
+        tpp = ctx.enter_context(tc.psum_pool(name="tpp", bufs=3))
         ctx.enter_context(tc.manual_schedule())
 
         warm = const.tile([P, 1], F32, name="warm")
@@ -64,16 +65,18 @@ def tile_quantumprocessinglayer_w_kernel(tc, x, W_words, W_scales, b, out):
                 out=wt[:].bitcast(I32),
                 in_=W_words[g].rearrange("p n t -> p (n t)").bitcast(I32),
             )
-            for j in range(4):
-                w_tiles[(g, j)] = wt[:, NT * j : NT * (j + 1)]
+            for ri, (c0, cw) in enumerate(RANGES):
+                w_tiles[(g, ri)] = wt[:, c0 : c0 + cw]
 
-        def load_w_piece(g, j):
-            wt = wpool.tile([P, NT], U32, name="w%d_%d" % (g, j), align_bytes=64)
+        def load_last_two(ri):
+            c0, cw = RANGES[ri]
+            wt = wpool.tile([P, 2, cw], U32, name="wl%d" % ri, align_bytes=64)
             nc.sync.dma_start(
                 out=wt[:].bitcast(I32),
-                in_=W_words[g][:, NT * j : NT * (j + 1), :].rearrange("p n t -> p (n t)").bitcast(I32),
+                in_=W_words[11::4, :, c0 : c0 + cw, :].rearrange("a p n t -> p a (n t)").bitcast(I32),
             )
-            w_tiles[(g, j)] = wt[:]
+            w_tiles[(11, ri)] = wt[:, 0, :]
+            w_tiles[(15, ri)] = wt[:, 1, :]
 
         def load_scales(c, q4):
             nc.sync.dma_start(
@@ -84,27 +87,26 @@ def tile_quantumprocessinglayer_w_kernel(tc, x, W_words, W_scales, b, out):
         g_order = [c + 4 * a for c in range(NCH) for a in range(4)]
         s_order = [(c, q4) for c in range(NCH) for q4 in (0, 2, 1, 3)]
         si = 0
-        for i, g in enumerate(g_order):
-            if i == len(g_order) - 1:
-                for j in range(4):
-                    load_w_piece(g, j)
-            else:
-                load_w(g)
+        for i, g in enumerate(g_order[:14]):
+            load_w(g)
             if i >= 1:
                 for r in range(SCALES_PER_W):
                     if si < len(s_order):
                         load_scales(s_order[si][0], s_order[si][1])
                         si += 1
+        for ri in range(len(RANGES)):
+            load_last_two(ri)
 
         xw = x_sb[:].bitcast(F32)
-        xts = []
-        for c in range(NCH):
+        xts = {}
+
+        def transposes(c):
             xt = tpp.tile([P, 2, 2, TOK], F32, name="xt%d" % c, tag="xt")
             for gi in range(2):
                 g = c + 4 * gi
                 for u in range(2):
                     nc.tensor.transpose(xt[:, gi, u, :], xw[:, 256 * g + u : 256 * (g + 1) : 2], ident[:])
-            xts.append(xt)
+            xts[c] = xt
 
         st = {}
 
@@ -148,30 +150,54 @@ def tile_quantumprocessinglayer_w_kernel(tc, x, W_words, W_scales, b, out):
             fb = st[c]
             nc.vector.quantize_mx(out=codes[:, c, :].bitcast(FP8X4), scales=fsc[:, c, :], in_=fb[:])
             if c == 0:
-                for j in range(4):
-                    accs.append(accp.tile([P, NT], F32, name="acc%d" % j, tag="acc%d" % j))
-            for a in range(4):
-                g = c + 4 * a
-                for j in range(4):
-                    nc.tensor.matmul_mx(
-                        out=accs[j][:],
-                        lhsT=codes[:, c, P * a : P * (a + 1)].bitcast(FP8X4),
-                        lhsT_scale=fsc[:, c, P * a : P * (a + 1)],
-                        rhs=w_tiles[(g, j)].bitcast(FP8X4),
-                        rhs_scale=planes[4 * a : P, c, NT * j : NT * (j + 1)],
-                        start=(c == 0 and a == 0),
-                        stop=(c == NCH - 1 and a == 3),
-                    )
+                for ri, (c0, cw) in enumerate(RANGES):
+                    accs.append(accp.tile([P, cw], F32, name="acc%d" % ri, tag="acc%d" % ri))
 
+            def mx(a, ri):
+                g = c + 4 * a
+                c0, cw = RANGES[ri]
+                nc.tensor.matmul_mx(
+                    out=accs[ri][:],
+                    lhsT=codes[:, c, P * a : P * (a + 1)].bitcast(FP8X4),
+                    lhsT_scale=fsc[:, c, P * a : P * (a + 1)],
+                    rhs=w_tiles[(g, ri)].bitcast(FP8X4),
+                    rhs_scale=planes[4 * a : P, c, c0 : c0 + cw],
+                    start=(c == 0 and a == 0),
+                    stop=(c == NCH - 1 and a == 3),
+                )
+
+            if c < NCH - 1:
+                for a in range(4):
+                    for ri in range(len(RANGES)):
+                        mx(a, ri)
+            else:
+                for a in range(2):
+                    for ri in range(len(RANGES)):
+                        mx(a, ri)
+                for ri in range(len(RANGES)):
+                    mx(2, ri)
+                    mx(3, ri)
+
+        transposes(0)
+        transposes(1)
+        transposes(2)
         copy_out(0, "v")
+        transposes(3)
         copy_out(1, "s")
         front(0)
         copy_out(2, "v")
         copy_out(3, "s")
         bps = []
-        for j in range(4):
-            bp = tpp.tile([P, NT], F32, name="bp%d" % j, tag="xt")
-            nc.tensor.matmul(bp[:], lhsT=ones[:], rhs=brow[:, NT * j : NT * (j + 1)], start=True, stop=True)
+        for h in range(2):
+            bp = tpp.tile([P, 2 * NT], BF16, name="bp%d" % h, tag="xt")
+            for j in range(2):
+                nc.tensor.matmul(
+                    bp[:, NT * j : NT * (j + 1)],
+                    lhsT=ones[:],
+                    rhs=brow[:, NT * (2 * h + j) : NT * (2 * h + j + 1)],
+                    start=True,
+                    stop=True,
+                )
             bps.append(bp)
         front(1)
         back_a(0)
@@ -184,11 +210,11 @@ def tile_quantumprocessinglayer_w_kernel(tc, x, W_words, W_scales, b, out):
         back_b(2)
         back_a(3)
         back_b(3)
-        for j in range(4):
-            nc.scalar.copy(out=bias_sb[:, NT * j : NT * (j + 1)], in_=bps[j][:])
+        for h in range(2):
+            nc.scalar.copy(out=bias_sb[:, 2 * NT * h : 2 * NT * (h + 1)], in_=bps[h][:])
 
-        for j in range(4):
-            js = slice(NT * j, NT * (j + 1))
-            nc.vector.tensor_tensor(out=bias_sb[:, js], in0=accs[j][:], in1=bias_sb[:, js], op=ALU.add)
+        for ri, (c0, cw) in enumerate(RANGES):
+            js = slice(c0, c0 + cw)
+            nc.vector.tensor_tensor(out=bias_sb[:, js], in0=accs[ri][:], in1=bias_sb[:, js], op=ALU.add)
             nc.scalar.activation(out=bias_sb[:, js], in_=bias_sb[:, js], func=ACT.Tanh)
             nc.sync.dma_start(out=out[0][:, js], in_=bias_sb[:, js])

@@ -22,7 +22,6 @@ U = 2048
 NT = 512
 NCH = 4
 CW = 1024
-SCALES_PER_W = 3
 RANGES = [(0, 512), (512, 512), (1024, 512), (1536, 256), (1792, 256)]
 
 
@@ -49,10 +48,10 @@ def tile_quantumprocessinglayer_w_kernel(tc, x, W_words, W_scales, b, out):
         fsc = const.tile([P, NCH, 512], U8, name="fsc", align_bytes=64)
 
         nc.sync.dma_start(out=x_sb[:], in_=x[0])
+        nc.vector.memset(planes[:].rearrange("p c n -> p (c n)").bitcast(I32), 0)
         nc.vector.memset(brow[:].bitcast(I32), 0)
         nc.vector.memset(warm[:], 0.0)
         nc.vector.memset(ones[:], 1.0)
-        nc.vector.memset(planes[:].rearrange("p c n -> p (c n)").bitcast(I32), 0)
         nc.scalar.dma_start(out=brow[0:1, :], in_=b.unsqueeze(0))
         nc.scalar.activation(out=warm_out[:], in_=warm[:], func=ACT.Silu)
         make_identity(nc, ident[:])
@@ -86,14 +85,10 @@ def tile_quantumprocessinglayer_w_kernel(tc, x, W_words, W_scales, b, out):
 
         g_order = [c + 4 * a for c in range(NCH) for a in range(4)]
         s_order = [(c, q4) for c in range(NCH) for q4 in (0, 2, 1, 3)]
-        si = 0
-        for i, g in enumerate(g_order[:14]):
+        for c, q4 in s_order:
+            load_scales(c, q4)
+        for g in g_order[:14]:
             load_w(g)
-            if i >= 1:
-                for r in range(SCALES_PER_W):
-                    if si < len(s_order):
-                        load_scales(s_order[si][0], s_order[si][1])
-                        si += 1
         for ri in range(len(RANGES)):
             load_last_two(ri)
 

@@ -52,7 +52,6 @@ def tile_quantumprocessinglayer_w_kernel(tc, x, W_words, W_scales, b, out):
         nc.vector.memset(brow[:].bitcast(I32), 0)
         nc.vector.memset(warm[:], 0.0)
         nc.vector.memset(ones[:], 1.0)
-        nc.scalar.dma_start(out=brow[0:1, :], in_=b.unsqueeze(0))
         nc.scalar.activation(out=warm_out[:], in_=warm[:], func=ACT.Silu)
         make_identity(nc, ident[:])
 
@@ -84,9 +83,10 @@ def tile_quantumprocessinglayer_w_kernel(tc, x, W_words, W_scales, b, out):
             )
 
         g_order = [c + 4 * a for c in range(NCH) for a in range(4)]
-        s_order = [(c, q4) for c in range(NCH) for q4 in (0, 2, 1, 3)]
+        s_order = [(c, q4) for q4 in (2, 3, 0, 1) for c in range(NCH)]
         for c, q4 in s_order:
             load_scales(c, q4)
+        nc.sync.dma_start(out=brow[0:1, :], in_=b.unsqueeze(0))
         for g in g_order[:14]:
             load_w(g)
         for ri in range(len(RANGES)):

@@ -52,6 +52,7 @@ def tile_quantumprocessinglayer_w_kernel(tc, x, W_words, W_scales, b, out):
         nc.vector.memset(brow[:].bitcast(I32), 0)
         nc.vector.memset(warm[:], 0.0)
         nc.vector.memset(ones[:], 1.0)
+        nc.scalar.dma_start(out=brow[0:1, :], in_=b.unsqueeze(0))
         nc.scalar.activation(out=warm_out[:], in_=warm[:], func=ACT.Silu)
         make_identity(nc, ident[:])
 
@@ -83,12 +84,14 @@ def tile_quantumprocessinglayer_w_kernel(tc, x, W_words, W_scales, b, out):
             )
 
         g_order = [c + 4 * a for c in range(NCH) for a in range(4)]
-        s_order = [(c, q4) for q4 in (2, 3, 0, 1) for c in range(NCH)]
-        for c, q4 in s_order:
-            load_scales(c, q4)
-        nc.sync.dma_start(out=brow[0:1, :], in_=b.unsqueeze(0))
-        for g in g_order[:14]:
+        for c in range(NCH):
+            load_scales(c, 2)
+            load_scales(c, 3)
+        for i, g in enumerate(g_order[:14]):
             load_w(g)
+            if i < NCH:
+                load_scales(i, 0)
+                load_scales(i, 1)
         for ri in range(len(RANGES)):
             load_last_two(ri)
 

@@ -88,10 +88,10 @@ def tile_quantumprocessinglayer_w_kernel(tc, x, W_words, W_scales, b, out):
             load_scales(c, 2)
             load_scales(c, 3)
         for i, g in enumerate(g_order[:14]):
-            load_w(g)
             if i < NCH:
                 load_scales(i, 0)
                 load_scales(i, 1)
+            load_w(g)
         for ri in range(len(RANGES)):
             load_last_two(ri)
 

import math
from contextlib import ExitStack

import concourse.mybir as mybir
from concourse.masks import make_identity

FLOPS = 2 * 128 * 8192 * 2048

FP8X4 = mybir.dt.float8_e4m3fn_x4
BF16 = mybir.dt.bfloat16
F32 = mybir.dt.float32
I32 = mybir.dt.int32
U32 = mybir.dt.uint32
U8 = mybir.dt.uint8
ACT = mybir.ActivationFunctionType
ALU = mybir.AluOpType

P = 128
TOK = 128
F = 4096
U = 2048
NT = 512
NCH = 4
CW = 1024
RANGES = [(0, 512), (512, 512), (1024, 512), (1536, 256), (1792, 256)]


def tile_quantumprocessinglayer_w_kernel(tc, x, W_words, W_scales, b, out):
    nc = tc.nc
    with ExitStack() as ctx:
        const = ctx.enter_context(tc.tile_pool(name="const", bufs=1))
        wpool = ctx.enter_context(tc.tile_pool(name="wpool", bufs=1))
        xgp = ctx.enter_context(tc.tile_pool(name="xgp", bufs=4))
        tmp = ctx.enter_context(tc.tile_pool(name="tmp", bufs=2))
        accp = ctx.enter_context(tc.psum_pool(name="accp", bufs=1))
        tpp = ctx.enter_context(tc.psum_pool(name="tpp", bufs=3))
        ctx.enter_context(tc.manual_schedule())

        warm = const.tile([P, 1], F32, name="warm")
        warm_out = const.tile([P, 1], F32, name="warm_out")
        brow = const.tile([P, U], BF16, name="brow")
        ones = const.tile([P, P], BF16, name="ones")
        planes = const.tile([P, NCH, U], U8, name="planes", align_bytes=64)
        ident = const.tile([P, P], F32, name="ident")
        x_sb = const.tile([P, F], BF16, name="x_sb")
        bias_sb = const.tile([P, U], F32, name="bias_sb")
        codes = const.tile([P, NCH, 512], U32, name="codes", align_bytes=64)
        fsc = const.tile([P, NCH, 512], U8, name="fsc", align_bytes=64)

        nc.sync.dma_start(out=x_sb[:], in_=x[0])
        nc.vector.memset(planes[:].rearrange("p c n -> p (c n)").bitcast(I32), 0)
        nc.vector.memset(brow[:].bitcast(I32), 0)
        nc.vector.memset(warm[:], 0.0)
        nc.vector.memset(ones[:], 1.0)
        nc.scalar.dma_start(out=brow[0:1, :], in_=b.unsqueeze(0))
        nc.scalar.activation(out=warm_out[:], in_=warm[:], func=ACT.Silu)
        make_identity(nc, ident[:])

        w_tiles = {}

        def load_w(g):
            wt = wpool.tile([P, U], U32, name="w%d" % g, align_bytes=64)
            nc.sync.dma_start(
                out=wt[:].bitcast(I32),
                in_=W_words[g].rearrange("p n t -> p (n t)").bitcast(I32),
            )
            for ri, (c0, cw) in enumerate(RANGES):
                w_tiles[(g, ri)] = wt[:, c0 : c0 + cw]

        def load_last_two(ri):
            c0, cw = RANGES[ri]
            wt = wpool.tile([P, 2, cw], U32, name="wl%d" % ri, align_bytes=64)
            nc.sync.dma_start(
                out=wt[:].bitcast(I32),
                in_=W_words[11::4, :, c0 : c0 + cw, :].rearrange("a p n t -> p a (n t)").bitcast(I32),
            )
            w_tiles[(11, ri)] = wt[:, 0, :]
            w_tiles[(15, ri)] = wt[:, 1, :]

        def load_scales(c, q4):
            nc.sync.dma_start(
                out=planes[32 * q4 : 32 * q4 + 16, c, :].bitcast(I32),
                in_=W_scales[c::4, 4 * q4 : 4 * q4 + 4, :].bitcast(I32),
            )

        g_order = [c + 4 * a for c in range(NCH) for a in range(4)]
        for c in range(NCH):
            load_scales(c, 2)
            load_scales(c, 3)
        for i, g in enumerate(g_order[:14]):
            if i < NCH:
                load_scales(i, 0)
                load_scales(i, 1)
            load_w(g)
        for ri in range(len(RANGES)):
            load_last_two(ri)

        xw = x_sb[:].bitcast(F32)
        xts = {}

        def transposes(c):
            xt = tpp.tile([P, 2, 2, TOK], F32, name="xt%d" % c, tag="xt")
            for gi in range(2):
                g = c + 4 * gi
                for u in range(2):
                    nc.tensor.transpose(xt[:, gi, u, :], xw[:, 256 * g + u : 256 * (g + 1) : 2], ident[:])
            xts[c] = xt

        st = {}

        xgs = {}

        def copy_out(c, eng):
            xg = xgp.tile([P, 2, TOK, 2], F32, name="xg%d" % c, tag="xg")
            src_ap = xts[c][:].rearrange("p g u r -> p g r u")
            if eng == "v":
                nc.vector.tensor_copy(out=xg[:], in_=src_ap)
            else:
                nc.scalar.copy(out=xg[:], in_=src_ap)
            xgs[c] = xg[:].rearrange("p g r u -> p (g r u)").bitcast(BF16)

        def front(c):
            xb = xgs[c]
            t_t = tmp.tile([P, CW], F32, name="t%d" % c, tag="t")
            nc.scalar.activation(out=t_t[:], in_=xb, func=ACT.Tanh, scale=2.0 * math.pi)
            k_t = tmp.tile([P, CW], I32, name="k%d" % c, tag="k")
            nc.vector.tensor_scalar(out=k_t[:], in0=xb, scalar1=0.5, scalar2=None, op0=ALU.mult)
            xr = tmp.tile([P, CW], BF16, name="xr%d" % c, tag="xr")
            nc.vector.scalar_tensor_tensor(out=xr[:], in0=k_t[:], scalar=-2.0, in1=xb, op0=ALU.mult, op1=ALU.add)
            s_t = tmp.tile([P, CW], F32, name="s%d" % c, tag="s")
            nc.scalar.activation(out=s_t[:], in_=xr[:], func=ACT.Sin, scale=math.pi)
            s2 = tmp.tile([P, CW], F32, name="ss%d" % c, tag="ss")
            nc.scalar.activation(out=s2[:], in_=s_t[:], func=ACT.Square)
            st[c] = (t_t, s_t, s2)

        def back_a(c):
            t_t, s_t, s2 = st[c]
            nc.vector.scalar_tensor_tensor(out=s2[:], in0=s2[:], scalar=1.0, in1=s_t[:], op0=ALU.subtract, op1=ALU.mult)
            nc.vector.scalar_tensor_tensor(out=t_t[:], in0=s2[:], scalar=-0.2, in1=t_t[:], op0=ALU.mult, op1=ALU.add)
            fb = tmp.tile([P, 2 * CW], BF16, name="fb%d" % c, tag="fb", align_bytes=64)
            nc.vector.tensor_copy(out=fb[:, 0:CW], in_=t_t[:])
            nc.scalar.activation(out=fb[:, CW : 2 * CW], in_=t_t[:], func=ACT.Square)
            st[c] = fb

        accs = []

        def back_b(c):
            fb = st[c]
            nc.vector.quantize_mx(out=codes[:, c, :].bitcast(FP8X4), scales=fsc[:, c, :], in_=fb[:])
            if c == 0:
                for ri, (c0, cw) in enumerate(RANGES):
                    accs.append(accp.tile([P, cw], F32, name="acc%d" % ri, tag="acc%d" % ri))

            def mx(a, ri):
                g = c + 4 * a
                c0, cw = RANGES[ri]
                nc.tensor.matmul_mx(
                    out=accs[ri][:],
                    lhsT=codes[:, c, P * a : P * (a + 1)].bitcast(FP8X4),
                    lhsT_scale=fsc[:, c, P * a : P * (a + 1)],
                    rhs=w_tiles[(g, ri)].bitcast(FP8X4),
                    rhs_scale=planes[4 * a : P, c, c0 : c0 + cw],
                    start=(c == 0 and a == 0),
                    stop=(c == NCH - 1 and a == 3),
                )

            if c < NCH - 1:
                for a in range(4):
                    for ri in range(len(RANGES)):
                        mx(a, ri)
            else:
                for a in range(2):
                    for ri in range(len(RANGES)):
                        mx(a, ri)
                for ri in range(len(RANGES)):
                    mx(2, ri)
                    mx(3, ri)

        transposes(0)
        transposes(1)
        transposes(2)
        copy_out(0, "v")
        transposes(3)
        copy_out(1, "s")
        front(0)
        copy_out(2, "v")
        copy_out(3, "s")
        bps = []
        for h in range(2):
            bp = tpp.tile([P, 2 * NT], BF16, name="bp%d" % h, tag="xt")
            for j in range(2):
                nc.tensor.matmul(
                    bp[:, NT * j : NT * (j + 1)],
                    lhsT=ones[:],
                    rhs=brow[:, NT * (2 * h + j) : NT * (2 * h + j + 1)],
                    start=True,
                    stop=True,
                )
            bps.append(bp)
        front(1)
        back_a(0)
        front(2)
        back_b(0)
        back_a(1)
        front(3)
        back_b(1)
        back_a(2)
        back_b(2)
        back_a(3)
        back_b(3)
        for h in range(2):
            nc.scalar.copy(out=bias_sb[:, 2 * NT * h : 2 * NT * (h + 1)], in_=bps[h][:])

        for ri, (c0, cw) in enumerate(RANGES):
            js = slice(c0, c0 + cw)
            nc.vector.tensor_tensor(out=bias_sb[:, js], in0=accs[ri][:], in1=bias_sb[:, js], op=ALU.add)
            nc.scalar.activation(out=bias_sb[:, js], in_=bias_sb[:, js], func=ACT.Tanh)
            nc.sync.dma_start(out=out[0][:, js], in_=bias_sb[:, js])
